import numpy as np
import ml_dtypes

BF16 = ml_dtypes.bfloat16


def bf(x):
    return np.asarray(x, np.float32).astype(BF16)


def f32(x):
    return np.asarray(x, np.float32)


def f64(x):
    return np.asarray(x).astype(np.float64)


def striped(idx):
    return np.tile(idx.reshape(-1, 16).T, (8, 1))


B, S, K, F, N, K2 = 512, 2048, 9, 448, 4032, 11


def setup_inputs():
    return {"p": f32(np.random.standard_normal((B, S))), "w1": f32(np.random.standard_normal((1, N)) / np.sqrt(F)), "b1": f32(np.random.uniform(0.3, 1.0, (1, K))), "w2": f32(np.random.uniform(0.2, 0.4, (1, K2))), "b2": f32(np.random.uniform(0.5, 1.0, (1,))), "offs": striped(np.random.permutation(np.tile(np.arange(S), 2))[:N])}


def reference(p, w1, b1, w2, b2, offs):
    idx = offs[:16].T.reshape(-1)
    p = f64(p)
    w2 = f64(w2)
    prod = p[:, idx] * f64(w1)
    s = prod.reshape(B, K, F).sum(axis=2) + f64(b1)
    age = p[:, -1:]
    female = p[:, -2:-1]
    return (s * w2[:, :K]).sum(axis=1, keepdims=True) + w2[0, -2] * age + w2[0, -1] * female + f64(b2)

@@ -1,0 +1,103 @@
+import concourse.mybir as mybir
+from concourse.masks import make_identity
+
+F32 = mybir.dt.float32
+U16 = mybir.dt.uint16
+MULT = mybir.AluOpType.mult
+ADD = mybir.AluOpType.add
+IDENTITY = mybir.ActivationFunctionType.Identity
+AXIS_X = mybir.AxisListType.X
+
+P = 128
+B, S = 512, 2048
+K, F = 9, 448
+N = K * F
+BLOCKS = B // P
+TERMS = K + 2
+OFFSET_COLUMNS = F // 16
+
+FLOPS = 2 * B * N
+
+
+def tile_pcgrimage_kernel(tc, p, w1, b1, w2, b2, offs, out):
+    nc = tc.nc
+    p_blocks = p.rearrange("(i q) s -> i q s", q=P)
+    out_rows = out.rearrange("(i q) o -> i (q o)", q=P)
+
+    with (
+        tc.tile_pool(name="held", bufs=1) as held,
+        tc.tile_pool(name="work", bufs=4) as work,
+        tc.psum_pool(name="psum", bufs=1) as psum,
+    ):
+        offsets = held.tile([P, N // 16], U16, name="offsets")
+        nc.sync.dma_start(offsets[:], offs)
+
+        w2_all = held.tile([P, TERMS], F32, name="w2_all")
+        nc.sync.dma_start(w2_all[:], w2.to_broadcast([P, TERMS]))
+        b1_all = held.tile([P, K], F32, name="b1_all")
+        nc.sync.dma_start(b1_all[:], b1.to_broadcast([P, K]))
+        b2_all = held.tile([P, 1], F32, name="b2_all")
+        nc.sync.dma_start(b2_all[:], b2.unsqueeze(0).to_broadcast([P, 1]))
+
+        window = [held.tile([P, S], F32, name=f"window{i}") for i in range(BLOCKS)]
+        w1_all = held.tile([P, N], F32, name="w1_all")
+        nc.sync.dma_start(w1_all[:, 0:F], w1[:, 0:F].to_broadcast([P, F]))
+        nc.sync.dma_start(window[0][:], p_blocks[0])
+        for k in range(1, K):
+            nc.sync.dma_start(
+                w1_all[:, k * F : (k + 1) * F], w1[:, k * F : (k + 1) * F].to_broadcast([P, F])
+            )
+        for i in range(1, BLOCKS):
+            nc.sync.dma_start(window[i][:], p_blocks[i])
+
+        identity = held.tile([P, P], F32, name="identity")
+        make_identity(nc, identity[:])
+
+        weighted_b1 = held.tile([P, K], F32, name="weighted_b1")
+        nc.vector.tensor_tensor(weighted_b1[:], w2_all[:, 0:K], b1_all[:], MULT)
+        bias_sum = held.tile([P, 1], F32, name="bias_sum")
+        nc.vector.tensor_reduce(bias_sum[:], weighted_b1[:], AXIS_X, ADD)
+
+        terms = held.tile([P, BLOCKS * TERMS], F32, name="terms")
+
+        for i in range(BLOCKS):
+            first = i * TERMS
+            nc.scalar.activation(
+                terms[:, first + K : first + K + 1],
+                window[i][:, S - 1 : S],
+                IDENTITY,
+                bias=bias_sum[:],
+                scale=w2_all[:, K : K + 1],
+            )
+            nc.scalar.activation(
+                terms[:, first + K + 1 : first + K + 2],
+                window[i][:, S - 2 : S - 1],
+                IDENTITY,
+                bias=b2_all[:],
+                scale=w2_all[:, K + 1 : K + 2],
+            )
+            for k in range(K):
+                product = work.tile([P, F], F32, name="product")
+                nc.vector.tensor_tensor(
+                    product[:],
+                    window[i][:].indirect(offsets[:, k * OFFSET_COLUMNS : (k + 1) * OFFSET_COLUMNS]),
+                    w1_all[:, k * F : (k + 1) * F],
+                    MULT,
+                )
+                nc.scalar.activation(
+                    product[:],
+                    product[:],
+                    IDENTITY,
+                    scale=w2_all[:, k : k + 1],
+                    accum_out=terms[:, first + k : first + k + 1],
+                )
+
+        total = held.tile([P, BLOCKS], F32, name="total")
+        nc.vector.tensor_reduce(
+            total[:], terms[:].rearrange("q (i t) -> q i t", t=TERMS), AXIS_X, ADD
+        )
+        total_turned = psum.tile([BLOCKS, P], F32, name="total_turned")
+        nc.tensor.transpose(total_turned[:], total[:], identity[:])
+        result = held.tile([BLOCKS, P], F32, name="result")
+        nc.vector.tensor_copy(result[:], total_turned[:])
+        nc.sync.dma_start(out_rows, result[:])

@@ -14,7 +14,8 @@ K, F = 9, 448
 N = K * F
 BLOCKS = B // P
 TERMS = K + 2
-OFFSET_COLUMNS = F // 16
+PIECES = (1, 4, 3, 1)
+assert sum(PIECES) == K and max(PIECES) * F <= S
 
 FLOPS = 2 * B * N
 
@@ -41,12 +42,16 @@ def tile_pcgrimage_kernel(tc, p, w1, b1, w2, b2, offs, out):
 
         window = [held.tile([P, S], F32, name=f"window{i}") for i in range(BLOCKS)]
         w1_all = held.tile([P, N], F32, name="w1_all")
-        nc.sync.dma_start(w1_all[:, 0:F], w1[:, 0:F].to_broadcast([P, F]))
-        nc.sync.dma_start(window[0][:], p_blocks[0])
-        for k in range(1, K):
+        piece_start = 0
+        for models in PIECES:
+            piece_end = piece_start + models * F
             nc.sync.dma_start(
-                w1_all[:, k * F : (k + 1) * F], w1[:, k * F : (k + 1) * F].to_broadcast([P, F])
+                w1_all[:, piece_start:piece_end],
+                w1[:, piece_start:piece_end].to_broadcast([P, piece_end - piece_start]),
             )
+            if piece_start == 0:
+                nc.sync.dma_start(window[0][:], p_blocks[0])
+            piece_start = piece_end
         for i in range(1, BLOCKS):
             nc.sync.dma_start(window[i][:], p_blocks[i])
 
@@ -76,21 +81,27 @@ def tile_pcgrimage_kernel(tc, p, w1, b1, w2, b2, offs, out):
                 bias=b2_all[:],
                 scale=w2_all[:, K + 1 : K + 2],
             )
-            for k in range(K):
-                product = work.tile([P, F], F32, name="product")
+            first_model = 0
+            for models in PIECES:
+                piece_start = first_model * F
+                piece_end = piece_start + models * F
+                product = work.tile([P, max(PIECES) * F], F32, name="product")
                 nc.vector.tensor_tensor(
-                    product[:],
-                    window[i][:].indirect(offsets[:, k * OFFSET_COLUMNS : (k + 1) * OFFSET_COLUMNS]),
-                    w1_all[:, k * F : (k + 1) * F],
+                    product[:, 0 : models * F],
+                    window[i][:].indirect(offsets[:, piece_start // 16 : piece_end // 16]),
+                    w1_all[:, piece_start:piece_end],
                     MULT,
                 )
-                nc.scalar.activation(
-                    product[:],
-                    product[:],
-                    IDENTITY,
-                    scale=w2_all[:, k : k + 1],
-                    accum_out=terms[:, first + k : first + k + 1],
-                )
+                for m in range(models):
+                    k = first_model + m
+                    nc.scalar.activation(
+                        product[:, m * F : (m + 1) * F],
+                        product[:, m * F : (m + 1) * F],
+                        IDENTITY,
+                        scale=w2_all[:, k : k + 1],
+                        accum_out=terms[:, first + k : first + k + 1],
+                    )
+                first_model += models
 
         total = held.tile([P, BLOCKS], F32, name="total")
         nc.vector.tensor_reduce(

@@ -14,7 +14,7 @@ K, F = 9, 448
 N = K * F
 BLOCKS = B // P
 TERMS = K + 2
-PIECES = (1, 4, 3, 1)
+PIECES = (1, 2, 3, 2, 1)
 assert sum(PIECES) == K and max(PIECES) * F <= S
 
 FLOPS = 2 * B * N

@@ -14,6 +14,7 @@ K, F = 9, 448
 N = K * F
 BLOCKS = B // P
 TERMS = K + 2
+SQUARE = 32
 PIECES = (1, 2, 3, 2, 1)
 assert sum(PIECES) == K and max(PIECES) * F <= S
 
@@ -33,15 +34,11 @@ def tile_pcgrimage_kernel(tc, p, w1, b1, w2, b2, offs, out):
         offsets = held.tile([P, N // 16], U16, name="offsets")
         nc.sync.dma_start(offsets[:], offs)
 
-        w2_all = held.tile([P, TERMS], F32, name="w2_all")
-        nc.sync.dma_start(w2_all[:], w2.to_broadcast([P, TERMS]))
-        b1_all = held.tile([P, K], F32, name="b1_all")
-        nc.sync.dma_start(b1_all[:], b1.to_broadcast([P, K]))
-        b2_all = held.tile([P, 1], F32, name="b2_all")
-        nc.sync.dma_start(b2_all[:], b2.unsqueeze(0).to_broadcast([P, 1]))
-
         window = [held.tile([P, S], F32, name=f"window{i}") for i in range(BLOCKS)]
         w1_all = held.tile([P, N], F32, name="w1_all")
+        w2_all = held.tile([P, TERMS], F32, name="w2_all")
+        b1_all = held.tile([P, K], F32, name="b1_all")
+        b2_all = held.tile([P, 1], F32, name="b2_all")
         piece_start = 0
         for models in PIECES:
             piece_end = piece_start + models * F
@@ -51,6 +48,9 @@ def tile_pcgrimage_kernel(tc, p, w1, b1, w2, b2, offs, out):
             )
             if piece_start == 0:
                 nc.sync.dma_start(window[0][:], p_blocks[0])
+                nc.sync.dma_start(w2_all[:], w2.to_broadcast([P, TERMS]))
+                nc.sync.dma_start(b1_all[:], b1.to_broadcast([P, K]))
+                nc.sync.dma_start(b2_all[:], b2.unsqueeze(0).to_broadcast([P, 1]))
             piece_start = piece_end
         for i in range(1, BLOCKS):
             nc.sync.dma_start(window[i][:], p_blocks[i])
@@ -59,11 +59,14 @@ def tile_pcgrimage_kernel(tc, p, w1, b1, w2, b2, offs, out):
         make_identity(nc, identity[:])
 
         weighted_b1 = held.tile([P, K], F32, name="weighted_b1")
-        nc.vector.tensor_tensor(weighted_b1[:], w2_all[:, 0:K], b1_all[:], MULT)
+        nc.gpsimd.tensor_tensor(weighted_b1[:], w2_all[:, 0:K], b1_all[:], MULT)
         bias_sum = held.tile([P, 1], F32, name="bias_sum")
-        nc.vector.tensor_reduce(bias_sum[:], weighted_b1[:], AXIS_X, ADD)
+        nc.scalar.activation(weighted_b1[:], weighted_b1[:], IDENTITY, accum_out=bias_sum[:])
 
         terms = held.tile([P, BLOCKS * TERMS], F32, name="terms")
+        early_total = held.tile([P, BLOCKS - 1], F32, name="early_total")
+        last_total = held.tile([P, SQUARE], F32, name="last_total", align_bytes=64)
+        nc.gpsimd.memset(last_total[:], 0.0)
 
         for i in range(BLOCKS):
             first = i * TERMS
@@ -103,12 +106,23 @@ def tile_pcgrimage_kernel(tc, p, w1, b1, w2, b2, offs, out):
                     )
                 first_model += models
 
-        total = held.tile([P, BLOCKS], F32, name="total")
-        nc.vector.tensor_reduce(
-            total[:], terms[:].rearrange("q (i t) -> q i t", t=TERMS), AXIS_X, ADD
+            if i < BLOCKS - 1:
+                nc.scalar.activation(
+                    terms[:, first : first + TERMS],
+                    terms[:, first : first + TERMS],
+                    IDENTITY,
+                    accum_out=early_total[:, i : i + 1],
+                )
+            if i == BLOCKS - 2:
+                early_turned = psum.tile([BLOCKS - 1, P], F32, name="early_turned")
+                nc.tensor.transpose(early_turned[:], early_total[:], identity[:])
+                early_result = held.tile([BLOCKS - 1, P], F32, name="early_result")
+                nc.scalar.copy(early_result[:], early_turned[:])
+                nc.sync.dma_start(out_rows[0 : BLOCKS - 1], early_result[:])
+
+        nc.vector.tensor_reduce(last_total[:, 0:1], terms[:, (BLOCKS - 1) * TERMS :], AXIS_X, ADD)
+        last_turned = held.tile([P, SQUARE], F32, name="last_turned", align_bytes=64)
+        nc.vector.transpose(last_turned[:], last_total[:])
+        nc.sync.dma_start(
+            out_rows[BLOCKS - 1].rearrange("(a c) -> a c", c=SQUARE), last_turned[0:P:SQUARE, :]
         )
-        total_turned = psum.tile([BLOCKS, P], F32, name="total_turned")
-        nc.tensor.transpose(total_turned[:], total[:], identity[:])
-        result = held.tile([BLOCKS, P], F32, name="result")
-        nc.vector.tensor_copy(result[:], total_turned[:])
-        nc.sync.dma_start(out_rows, result[:])

@@ -4,21 +4,34 @@ from concourse.masks import make_identity
 F32 = mybir.dt.float32
 U16 = mybir.dt.uint16
 MULT = mybir.AluOpType.mult
-ADD = mybir.AluOpType.add
 IDENTITY = mybir.ActivationFunctionType.Identity
-AXIS_X = mybir.AxisListType.X
 
 P = 128
 B, S = 512, 2048
 K, F = 9, 448
 N = K * F
 BLOCKS = B // P
-TERMS = K + 2
 SQUARE = 32
-PIECES = (1, 2, 3, 2, 1)
-assert sum(PIECES) == K and max(PIECES) * F <= S
+PIECES = (F, 2 * F, 3 * F, 2 * F, F)
+FIRST_PIECES = (128, 256, 512, 2 * F, 3 * F, 2 * F)
+LAST_PIECES = (F, 2 * F, 3 * F, F, F, 256, 192)
+CLOSING = LAST_PIECES[-1]
+assert CLOSING <= F
+LONGEST = max(FIRST_PIECES + PIECES + LAST_PIECES)
+assert sum(FIRST_PIECES) == N and sum(PIECES) == N and sum(LAST_PIECES) == N and LONGEST <= S
+assert all(length % 32 == 0 for length in FIRST_PIECES + PIECES + LAST_PIECES)
 
 FLOPS = 2 * B * N
+
+
+def spans(lengths):
+    ends = [sum(lengths[: n + 1]) for n in range(len(lengths))]
+    return [(end - length, end) for end, length in zip(ends, lengths)]
+
+
+def model_parts(start, end):
+    bounds = [start] + [bound for bound in range(0, N, F) if start < bound < end] + [end]
+    return list(zip(bounds[:-1], bounds[1:]))
 
 
 def tile_pcgrimage_kernel(tc, p, w1, b1, w2, b2, offs, out):
@@ -28,30 +41,25 @@ def tile_pcgrimage_kernel(tc, p, w1, b1, w2, b2, offs, out):
 
     with (
         tc.tile_pool(name="held", bufs=1) as held,
-        tc.tile_pool(name="work", bufs=4) as work,
+        tc.tile_pool(name="work", bufs=8) as work,
         tc.psum_pool(name="psum", bufs=1) as psum,
     ):
         offsets = held.tile([P, N // 16], U16, name="offsets")
-        nc.sync.dma_start(offsets[:], offs)
-
         window = [held.tile([P, S], F32, name=f"window{i}") for i in range(BLOCKS)]
         w1_all = held.tile([P, N], F32, name="w1_all")
-        w2_all = held.tile([P, TERMS], F32, name="w2_all")
+        w2_all = held.tile([P, K + 2], F32, name="w2_all")
         b1_all = held.tile([P, K], F32, name="b1_all")
         b2_all = held.tile([P, 1], F32, name="b2_all")
-        piece_start = 0
-        for models in PIECES:
-            piece_end = piece_start + models * F
-            nc.sync.dma_start(
-                w1_all[:, piece_start:piece_end],
-                w1[:, piece_start:piece_end].to_broadcast([P, piece_end - piece_start]),
-            )
-            if piece_start == 0:
+
+        nc.sync.dma_start(offsets[:], offs)
+        for start, end in spans(FIRST_PIECES):
+            nc.sync.dma_start(w1_all[:, start:end], w1[:, start:end].to_broadcast([P, end - start]))
+            if start == 0:
                 nc.sync.dma_start(window[0][:], p_blocks[0])
-                nc.sync.dma_start(w2_all[:], w2.to_broadcast([P, TERMS]))
+            if start == FIRST_PIECES[0]:
+                nc.sync.dma_start(w2_all[:], w2.to_broadcast([P, K + 2]))
                 nc.sync.dma_start(b1_all[:], b1.to_broadcast([P, K]))
                 nc.sync.dma_start(b2_all[:], b2.unsqueeze(0).to_broadcast([P, 1]))
-            piece_start = piece_end
         for i in range(1, BLOCKS):
             nc.sync.dma_start(window[i][:], p_blocks[i])
 
@@ -63,66 +71,71 @@ def tile_pcgrimage_kernel(tc, p, w1, b1, w2, b2, offs, out):
         bias_sum = held.tile([P, 1], F32, name="bias_sum")
         nc.scalar.activation(weighted_b1[:], weighted_b1[:], IDENTITY, accum_out=bias_sum[:])
 
-        terms = held.tile([P, BLOCKS * TERMS], F32, name="terms")
+        w1_closing = held.tile([P, CLOSING], F32, name="w1_closing")
+        nc.scalar.activation(
+            w1_closing[:], w1_all[:, N - CLOSING : N], IDENTITY, scale=w2_all[:, K - 1 : K]
+        )
+
         early_total = held.tile([P, BLOCKS - 1], F32, name="early_total")
         last_total = held.tile([P, SQUARE], F32, name="last_total", align_bytes=64)
         nc.gpsimd.memset(last_total[:], 0.0)
 
         for i in range(BLOCKS):
-            first = i * TERMS
+            last_block = i == BLOCKS - 1
+            pieces = spans(FIRST_PIECES if i == 0 else LAST_PIECES[:-1] if last_block else PIECES)
+            sums = sum(len(model_parts(start, end)) for start, end in pieces)
+            terms = held.tile([P, 2 + sums + (CLOSING if last_block else 0)], F32, name=f"terms{i}")
             nc.scalar.activation(
-                terms[:, first + K : first + K + 1],
+                terms[:, 0:1],
                 window[i][:, S - 1 : S],
                 IDENTITY,
                 bias=bias_sum[:],
                 scale=w2_all[:, K : K + 1],
             )
             nc.scalar.activation(
-                terms[:, first + K + 1 : first + K + 2],
+                terms[:, 1:2],
                 window[i][:, S - 2 : S - 1],
                 IDENTITY,
                 bias=b2_all[:],
                 scale=w2_all[:, K + 1 : K + 2],
             )
-            first_model = 0
-            for models in PIECES:
-                piece_start = first_model * F
-                piece_end = piece_start + models * F
-                product = work.tile([P, max(PIECES) * F], F32, name="product")
+            column = 2
+            for start, end in pieces:
+                product = work.tile([P, LONGEST], F32, name="product")
                 nc.vector.tensor_tensor(
-                    product[:, 0 : models * F],
-                    window[i][:].indirect(offsets[:, piece_start // 16 : piece_end // 16]),
-                    w1_all[:, piece_start:piece_end],
+                    product[:, 0 : end - start],
+                    window[i][:].indirect(offsets[:, start // 16 : end // 16]),
+                    w1_all[:, start:end],
                     MULT,
                 )
-                for m in range(models):
-                    k = first_model + m
+                for part_start, part_end in model_parts(start, end):
+                    k = part_start // F
                     nc.scalar.activation(
-                        product[:, m * F : (m + 1) * F],
-                        product[:, m * F : (m + 1) * F],
+                        product[:, part_start - start : part_end - start],
+                        product[:, part_start - start : part_end - start],
                         IDENTITY,
                         scale=w2_all[:, k : k + 1],
-                        accum_out=terms[:, first + k : first + k + 1],
+                        accum_out=terms[:, column : column + 1],
                     )
-                first_model += models
-
-            if i < BLOCKS - 1:
-                nc.scalar.activation(
-                    terms[:, first : first + TERMS],
-                    terms[:, first : first + TERMS],
-                    IDENTITY,
-                    accum_out=early_total[:, i : i + 1],
-                )
+                    column += 1
+            if not last_block:
+                nc.scalar.activation(terms[:], terms[:], IDENTITY, accum_out=early_total[:, i : i + 1])
             if i == BLOCKS - 2:
                 early_turned = psum.tile([BLOCKS - 1, P], F32, name="early_turned")
                 nc.tensor.transpose(early_turned[:], early_total[:], identity[:])
                 early_result = held.tile([BLOCKS - 1, P], F32, name="early_result")
                 nc.scalar.copy(early_result[:], early_turned[:])
                 nc.sync.dma_start(out_rows[0 : BLOCKS - 1], early_result[:])
-
-        nc.vector.tensor_reduce(last_total[:, 0:1], terms[:, (BLOCKS - 1) * TERMS :], AXIS_X, ADD)
-        last_turned = held.tile([P, SQUARE], F32, name="last_turned", align_bytes=64)
-        nc.vector.transpose(last_turned[:], last_total[:])
-        nc.sync.dma_start(
-            out_rows[BLOCKS - 1].rearrange("(a c) -> a c", c=SQUARE), last_turned[0:P:SQUARE, :]
-        )
+            if last_block:
+                nc.vector.tensor_tensor(
+                    terms[:, column:],
+                    window[i][:].indirect(offsets[:, (N - CLOSING) // 16 :]),
+                    w1_closing[:],
+                    MULT,
+                )
+                nc.scalar.activation(terms[:], terms[:], IDENTITY, accum_out=last_total[:, 0:1])
+                last_turned = held.tile([P, SQUARE], F32, name="last_turned", align_bytes=64)
+                nc.vector.transpose(last_turned[:], last_total[:])
+                nc.sync.dma_start(
+                    out_rows[i].rearrange("(a c) -> a c", c=SQUARE), last_turned[0:P:SQUARE, :]
+                )

@@ -12,7 +12,7 @@ K, F = 9, 448
 N = K * F
 BLOCKS = B // P
 SQUARE = 32
-PIECES = (F, 2 * F, 3 * F, 2 * F, F)
+PIECES = (N // 2, N // 2)
 FIRST_PIECES = (128, 256, 512, 2 * F, 3 * F, 2 * F)
 LAST_PIECES = (F, 2 * F, 3 * F, F, F, 256, 192)
 CLOSING = LAST_PIECES[-1]

@@ -11,9 +11,12 @@ B, S = 512, 2048
 K, F = 9, 448
 N = K * F
 BLOCKS = B // P
+BANK = 512
 SQUARE = 32
 PIECES = (N // 2, N // 2)
 FIRST_PIECES = (128, 256, 512, 2 * F, 3 * F, 2 * F)
+ROW_PIECES = FIRST_PIECES[:2]
+ROW = sum(ROW_PIECES)
 LAST_PIECES = (F, 2 * F, 3 * F, F, F, 256, 192)
 CLOSING = LAST_PIECES[-1]
 assert CLOSING <= F
@@ -47,21 +50,28 @@ def tile_pcgrimage_kernel(tc, p, w1, b1, w2, b2, offs, out):
         offsets = held.tile([P, N // 16], U16, name="offsets")
         window = [held.tile([P, S], F32, name=f"window{i}") for i in range(BLOCKS)]
         w1_all = held.tile([P, N], F32, name="w1_all")
+        w1_row = held.tile([1, ROW], F32, name="w1_row")
+        ones = held.tile([1, P], F32, name="ones")
         w2_all = held.tile([P, K + 2], F32, name="w2_all")
         b1_all = held.tile([P, K], F32, name="b1_all")
         b2_all = held.tile([P, 1], F32, name="b2_all")
 
+        nc.sync.dma_start(w1_row[:], w1[:, 0:ROW])
         nc.sync.dma_start(offsets[:], offs)
-        for start, end in spans(FIRST_PIECES):
+        nc.sync.dma_start(window[0][:], p_blocks[0])
+        nc.sync.dma_start(w2_all[:], w2.to_broadcast([P, K + 2]))
+        nc.sync.dma_start(b1_all[:], b1.to_broadcast([P, K]))
+        nc.sync.dma_start(b2_all[:], b2.unsqueeze(0).to_broadcast([P, 1]))
+        for start, end in spans(FIRST_PIECES)[len(ROW_PIECES) :]:
             nc.sync.dma_start(w1_all[:, start:end], w1[:, start:end].to_broadcast([P, end - start]))
-            if start == 0:
-                nc.sync.dma_start(window[0][:], p_blocks[0])
-            if start == FIRST_PIECES[0]:
-                nc.sync.dma_start(w2_all[:], w2.to_broadcast([P, K + 2]))
-                nc.sync.dma_start(b1_all[:], b1.to_broadcast([P, K]))
-                nc.sync.dma_start(b2_all[:], b2.unsqueeze(0).to_broadcast([P, 1]))
         for i in range(1, BLOCKS):
             nc.sync.dma_start(window[i][:], p_blocks[i])
+
+        nc.vector.memset(ones[:], 1.0)
+        for start, end in spans(ROW_PIECES):
+            w1_spread = psum.tile([P, BANK], F32, name=f"w1_spread{start}")
+            nc.tensor.matmul(w1_spread[:, 0 : end - start], ones[:], w1_row[:, start:end], start=True, stop=True)
+            nc.scalar.copy(w1_all[:, start:end], w1_spread[:, 0 : end - start])
 
         identity = held.tile([P, P], F32, name="identity")
         make_identity(nc, identity[:])

@@ -17,7 +17,8 @@ PIECES = (N // 2, N // 2)
 FIRST_PIECES = (128, 256, 512, 2 * F, 3 * F, 2 * F)
 ROW_PIECES = FIRST_PIECES[:2]
 ROW = sum(ROW_PIECES)
-LAST_PIECES = (F, 2 * F, 3 * F, F, F, 256, 192)
+LAST_PIECES = (1920, 1024, 576, 320, 192)
+EARLY_ENDS = {1: 0, 2: 2}
 CLOSING = LAST_PIECES[-1]
 assert CLOSING <= F
 LONGEST = max(FIRST_PIECES + PIECES + LAST_PIECES)
@@ -130,12 +131,13 @@ def tile_pcgrimage_kernel(tc, p, w1, b1, w2, b2, offs, out):
                     column += 1
             if not last_block:
                 nc.scalar.activation(terms[:], terms[:], IDENTITY, accum_out=early_total[:, i : i + 1])
-            if i == BLOCKS - 2:
-                early_turned = psum.tile([BLOCKS - 1, P], F32, name="early_turned")
-                nc.tensor.transpose(early_turned[:], early_total[:], identity[:])
-                early_result = held.tile([BLOCKS - 1, P], F32, name="early_result")
+            if i in EARLY_ENDS:
+                first = EARLY_ENDS[i]
+                early_turned = psum.tile([i + 1 - first, P], F32, name=f"early_turned{i}")
+                nc.tensor.transpose(early_turned[:], early_total[:, first : i + 1], identity[:])
+                early_result = held.tile([i + 1 - first, P], F32, name=f"early_result{i}")
                 nc.scalar.copy(early_result[:], early_turned[:])
-                nc.sync.dma_start(out_rows[0 : BLOCKS - 1], early_result[:])
+                nc.sync.dma_start(out_rows[first : i + 1], early_result[:])
             if last_block:
                 nc.vector.tensor_tensor(
                     terms[:, column:],

@@ -14,9 +14,9 @@ BLOCKS = B // P
 BANK = 512
 SQUARE = 32
 PIECES = (N // 2, N // 2)
-FIRST_PIECES = (128, 256, 512, 2 * F, 3 * F, 2 * F)
-ROW_PIECES = FIRST_PIECES[:2]
-ROW = sum(ROW_PIECES)
+FIRST_PIECES = (384, 512, 1120, 2016)
+ROW = FIRST_PIECES[0]
+HALF = ROW // 2
 LAST_PIECES = (1920, 1024, 576, 320, 192)
 EARLY_ENDS = {1: 0, 2: 2}
 CLOSING = LAST_PIECES[-1]
@@ -60,16 +60,17 @@ def tile_pcgrimage_kernel(tc, p, w1, b1, w2, b2, offs, out):
         nc.sync.dma_start(w1_row[:], w1[:, 0:ROW])
         nc.sync.dma_start(offsets[:], offs)
         nc.sync.dma_start(window[0][:], p_blocks[0])
-        nc.sync.dma_start(w2_all[:], w2.to_broadcast([P, K + 2]))
-        nc.sync.dma_start(b1_all[:], b1.to_broadcast([P, K]))
-        nc.sync.dma_start(b2_all[:], b2.unsqueeze(0).to_broadcast([P, 1]))
-        for start, end in spans(FIRST_PIECES)[len(ROW_PIECES) :]:
+        for start, end in spans(FIRST_PIECES)[1:]:
+            if end == N:
+                nc.sync.dma_start(w2_all[:], w2.to_broadcast([P, K + 2]))
+                nc.sync.dma_start(b1_all[:], b1.to_broadcast([P, K]))
+                nc.sync.dma_start(b2_all[:], b2.unsqueeze(0).to_broadcast([P, 1]))
             nc.sync.dma_start(w1_all[:, start:end], w1[:, start:end].to_broadcast([P, end - start]))
         for i in range(1, BLOCKS):
             nc.sync.dma_start(window[i][:], p_blocks[i])
 
         nc.vector.memset(ones[:], 1.0)
-        for start, end in spans(ROW_PIECES):
+        for start, end in spans((HALF, HALF)):
             w1_spread = psum.tile([P, BANK], F32, name=f"w1_spread{start}")
             nc.tensor.matmul(w1_spread[:, 0 : end - start], ones[:], w1_row[:, start:end], start=True, stop=True)
             nc.scalar.copy(w1_all[:, start:end], w1_spread[:, 0 : end - start])

@@ -79,7 +79,10 @@ def tile_pcgrimage_kernel(tc, p, w1, b1, w2, b2, offs, out):
         make_identity(nc, identity[:])
 
         weighted_b1 = held.tile([P, K], F32, name="weighted_b1")
-        nc.gpsimd.tensor_tensor(weighted_b1[:], w2_all[:, 0:K], b1_all[:], MULT)
+        for k in range(K):
+            nc.scalar.activation(
+                weighted_b1[:, k : k + 1], b1_all[:, k : k + 1], IDENTITY, scale=w2_all[:, k : k + 1]
+            )
         bias_sum = held.tile([P, 1], F32, name="bias_sum")
         nc.scalar.activation(weighted_b1[:], weighted_b1[:], IDENTITY, accum_out=bias_sum[:])
 

import concourse.mybir as mybir
from concourse.masks import make_identity

F32 = mybir.dt.float32
U16 = mybir.dt.uint16
MULT = mybir.AluOpType.mult
IDENTITY = mybir.ActivationFunctionType.Identity

P = 128
B, S = 512, 2048
K, F = 9, 448
N = K * F
BLOCKS = B // P
BANK = 512
SQUARE = 32
PIECES = (N // 2, N // 2)
FIRST_PIECES = (384, 512, 1120, 2016)
ROW = FIRST_PIECES[0]
HALF = ROW // 2
LAST_PIECES = (1920, 1024, 576, 320, 192)
EARLY_ENDS = {1: 0, 2: 2}
CLOSING = LAST_PIECES[-1]
assert CLOSING <= F
LONGEST = max(FIRST_PIECES + PIECES + LAST_PIECES)
assert sum(FIRST_PIECES) == N and sum(PIECES) == N and sum(LAST_PIECES) == N and LONGEST <= S
assert all(length % 32 == 0 for length in FIRST_PIECES + PIECES + LAST_PIECES)

FLOPS = 2 * B * N


def spans(lengths):
    ends = [sum(lengths[: n + 1]) for n in range(len(lengths))]
    return [(end - length, end) for end, length in zip(ends, lengths)]


def model_parts(start, end):
    bounds = [start] + [bound for bound in range(0, N, F) if start < bound < end] + [end]
    return list(zip(bounds[:-1], bounds[1:]))


def tile_pcgrimage_kernel(tc, p, w1, b1, w2, b2, offs, out):
    nc = tc.nc
    p_blocks = p.rearrange("(i q) s -> i q s", q=P)
    out_rows = out.rearrange("(i q) o -> i (q o)", q=P)

    with (
        tc.tile_pool(name="held", bufs=1) as held,
        tc.tile_pool(name="work", bufs=8) as work,
        tc.psum_pool(name="psum", bufs=1) as psum,
    ):
        offsets = held.tile([P, N // 16], U16, name="offsets")
        window = [held.tile([P, S], F32, name=f"window{i}") for i in range(BLOCKS)]
        w1_all = held.tile([P, N], F32, name="w1_all")
        w1_row = held.tile([1, ROW], F32, name="w1_row")
        ones = held.tile([1, P], F32, name="ones")
        w2_all = held.tile([P, K + 2], F32, name="w2_all")
        b1_all = held.tile([P, K], F32, name="b1_all")
        b2_all = held.tile([P, 1], F32, name="b2_all")

        nc.sync.dma_start(w1_row[:], w1[:, 0:ROW])
        nc.sync.dma_start(offsets[:], offs)
        nc.sync.dma_start(window[0][:], p_blocks[0])
        for start, end in spans(FIRST_PIECES)[1:]:
            if end == N:
                nc.sync.dma_start(w2_all[:], w2.to_broadcast([P, K + 2]))
                nc.sync.dma_start(b1_all[:], b1.to_broadcast([P, K]))
                nc.sync.dma_start(b2_all[:], b2.unsqueeze(0).to_broadcast([P, 1]))
            nc.sync.dma_start(w1_all[:, start:end], w1[:, start:end].to_broadcast([P, end - start]))
        for i in range(1, BLOCKS):
            nc.sync.dma_start(window[i][:], p_blocks[i])

        nc.vector.memset(ones[:], 1.0)
        for start, end in spans((HALF, HALF)):
            w1_spread = psum.tile([P, BANK], F32, name=f"w1_spread{start}")
            nc.tensor.matmul(w1_spread[:, 0 : end - start], ones[:], w1_row[:, start:end], start=True, stop=True)
            nc.scalar.copy(w1_all[:, start:end], w1_spread[:, 0 : end - start])

        identity = held.tile([P, P], F32, name="identity")
        make_identity(nc, identity[:])

        weighted_b1 = held.tile([P, K], F32, name="weighted_b1")
        for k in range(K):
            nc.scalar.activation(
                weighted_b1[:, k : k + 1], b1_all[:, k : k + 1], IDENTITY, scale=w2_all[:, k : k + 1]
            )
        bias_sum = held.tile([P, 1], F32, name="bias_sum")
        nc.scalar.activation(weighted_b1[:], weighted_b1[:], IDENTITY, accum_out=bias_sum[:])

        w1_closing = held.tile([P, CLOSING], F32, name="w1_closing")
        nc.scalar.activation(
            w1_closing[:], w1_all[:, N - CLOSING : N], IDENTITY, scale=w2_all[:, K - 1 : K]
        )

        early_total = held.tile([P, BLOCKS - 1], F32, name="early_total")
        last_total = held.tile([P, SQUARE], F32, name="last_total", align_bytes=64)
        nc.gpsimd.memset(last_total[:], 0.0)

        for i in range(BLOCKS):
            last_block = i == BLOCKS - 1
            pieces = spans(FIRST_PIECES if i == 0 else LAST_PIECES[:-1] if last_block else PIECES)
            sums = sum(len(model_parts(start, end)) for start, end in pieces)
            terms = held.tile([P, 2 + sums + (CLOSING if last_block else 0)], F32, name=f"terms{i}")
            nc.scalar.activation(
                terms[:, 0:1],
                window[i][:, S - 1 : S],
                IDENTITY,
                bias=bias_sum[:],
                scale=w2_all[:, K : K + 1],
            )
            nc.scalar.activation(
                terms[:, 1:2],
                window[i][:, S - 2 : S - 1],
                IDENTITY,
                bias=b2_all[:],
                scale=w2_all[:, K + 1 : K + 2],
            )
            column = 2
            for start, end in pieces:
                product = work.tile([P, LONGEST], F32, name="product")
                nc.vector.tensor_tensor(
                    product[:, 0 : end - start],
                    window[i][:].indirect(offsets[:, start // 16 : end // 16]),
                    w1_all[:, start:end],
                    MULT,
                )
                for part_start, part_end in model_parts(start, end):
                    k = part_start // F
                    nc.scalar.activation(
                        product[:, part_start - start : part_end - start],
                        product[:, part_start - start : part_end - start],
                        IDENTITY,
                        scale=w2_all[:, k : k + 1],
                        accum_out=terms[:, column : column + 1],
                    )
                    column += 1
            if not last_block:
                nc.scalar.activation(terms[:], terms[:], IDENTITY, accum_out=early_total[:, i : i + 1])
            if i in EARLY_ENDS:
                first = EARLY_ENDS[i]
                early_turned = psum.tile([i + 1 - first, P], F32, name=f"early_turned{i}")
                nc.tensor.transpose(early_turned[:], early_total[:, first : i + 1], identity[:])
                early_result = held.tile([i + 1 - first, P], F32, name=f"early_result{i}")
                nc.scalar.copy(early_result[:], early_turned[:])
                nc.sync.dma_start(out_rows[first : i + 1], early_result[:])
            if last_block:
                nc.vector.tensor_tensor(
                    terms[:, column:],
                    window[i][:].indirect(offsets[:, (N - CLOSING) // 16 :]),
                    w1_closing[:],
                    MULT,
                )
                nc.scalar.activation(terms[:], terms[:], IDENTITY, accum_out=last_total[:, 0:1])
                last_turned = held.tile([P, SQUARE], F32, name="last_turned", align_bytes=64)
                nc.vector.transpose(last_turned[:], last_total[:])
                nc.sync.dma_start(
                    out_rows[i].rearrange("(a c) -> a c", c=SQUARE), last_turned[0:P:SQUARE, :]
                )
